import numpy as np
import ml_dtypes


def mxq(x, axis, fmt="e4m3"):
    dtype, down = {"e4m3": (ml_dtypes.float8_e4m3fn, 7), "e5m2": (ml_dtypes.float8_e5m2, 14)}[fmt]
    v = np.moveaxis(np.asarray(x, np.float32).astype(ml_dtypes.bfloat16).astype(np.float64), axis, -1)
    blocks = v.reshape(v.shape[:-1] + (-1, 32))
    amax = np.abs(blocks).max(-1, keepdims=True)
    byte = np.maximum(np.where(amax > 0, np.frexp(amax)[1] - 1 + 127, 0) - down, 1)
    scale = np.exp2(byte - 127.0)
    codes = (blocks / scale).astype(np.float32).astype(dtype).astype(np.float64)
    return np.moveaxis((codes * scale).reshape(v.shape), -1, axis)


WIDE = False


def mx_kscale(k):
    if not WIDE:
        return np.ones(k)
    levels = np.array([10, -10, 5, -5, 0])
    a = np.random.permutation(np.resize(levels, k // 512 * 4)).reshape(k // 512, 4)
    idx = np.arange(k)
    return np.exp2(a[idx // 512, idx % 128 // 32])


BF16 = ml_dtypes.bfloat16


def bf(x):
    return np.asarray(x, np.float32).astype(BF16)


def f64(x):
    return np.asarray(x).astype(np.float64)


B, S, D, F, N = 8, 1024, 512, 512, 256
SPARSITY = 0.1


def make_theta_sign(d1, d2, gain, row, col):
    mask = np.random.random((d1, d2)) < SPARSITY
    mag = np.abs(np.random.standard_normal((d1, d2))) * gain / np.sqrt(SPARSITY * d1)
    th = np.where(mask, mag, -mag) / row[:, None] * col
    sign = np.where(np.random.random((d1, d2)) < 0.5, -1.0, 1.0)
    return bf(th), bf(sign)


def setup_inputs():
    s, t = mx_kscale(D), mx_kscale(F)
    x = bf(np.random.standard_normal((B, S, D)) * s)
    th1, sign1 = make_theta_sign(D, F, 1.0, s, t)
    th2, sign2 = make_theta_sign(F, N, 1.4, t, np.ones(N))
    return {"x": x, "th1": th1, "sign1": sign1, "th2": th2, "sign2": sign2, "relu": 1}


def reference(x, th1, sign1, th2, sign2, relu):
    x = f64(x)
    for th, sign in ((f64(th1), f64(sign1)), (f64(th2), f64(sign2))):
        w = th * sign * (th > 0)
        x = mxq(x, 2, "e4m3") @ mxq(w, 0, "e4m3")
        if relu:
            x = np.maximum(x, 0.0)
    return x

@@ -1,0 +1,221 @@
+from contextlib import ExitStack
+
+import concourse.masks as masks
+import concourse.mybir as mybir
+
+F32 = mybir.dt.float32
+BF16 = mybir.dt.bfloat16
+U32 = mybir.dt.uint32
+U8 = mybir.dt.uint8
+FP8X4 = mybir.dt.float8_e4m3fn_x4
+ALU = mybir.AluOpType
+ACT = mybir.ActivationFunctionType
+
+P = 128
+TOKENS = 8192
+D = 512
+F = 512
+N = 256
+TILES = TOKENS // P
+RT = 4
+R = TILES // RT
+LEAD = 3
+MANUAL = True
+
+FLOPS = 2 * TOKENS * D * (F + N)
+
+
+def tile_sparse_connect_t_kernel(tc, x, th1, sign1, th2, sign2, relu, out):
+    assert relu == 1
+    nc = tc.nc
+    xv = x.flatten_outer_dims().rearrange("(p j) k -> p (j k)", j=TILES)
+    ov = out.flatten_outer_dims().rearrange("(p j) n -> p (j n)", j=TILES)
+
+    with ExitStack() as ctx:
+        if MANUAL:
+            ctx.enter_context(tc.manual_schedule())
+        const = ctx.enter_context(tc.tile_pool(name="const", bufs=1))
+        ring = ctx.enter_context(tc.tile_pool(name="ring", bufs=3))
+        tpool = ctx.enter_context(tc.psum_pool(name="tpool", bufs=2))
+        hpool = ctx.enter_context(tc.psum_pool(name="hpool", bufs=4))
+        opool = ctx.enter_context(tc.psum_pool(name="opool", bufs=2))
+
+        t1 = const.tile([P, 4 * F], BF16, name="t1")
+        s1 = const.tile([P, 4 * F], BF16, name="s1")
+        t2 = const.tile([P, 4 * N], BF16, name="t2")
+        s2 = const.tile([P, 4 * N], BF16, name="s2")
+        xs = [const.tile([P, RT * D], BF16, name="xs%d" % r) for r in range(R)]
+        ob = [const.tile([P, RT * N], F32, name="ob%d" % r) for r in range(R)]
+
+        def load_w1(dst, src):
+            nc.sync.dma_start(
+                out=dst[:].rearrange("p (u c) -> p u c", u=2),
+                in_=src.rearrange("(u p e) f -> p u (e f)", u=2, p=P, e=2),
+            )
+
+        def load_x(r):
+            nc.sync.dma_start(out=xs[r][:], in_=xv[:, r * RT * D : (r + 1) * RT * D])
+
+        load_w1(t1, th1)
+        load_w1(s1, sign1)
+        for r in range(3):
+            load_x(r)
+        nc.sync.dma_start(out=t2[:], in_=th2.rearrange("(p t) n -> p (t n)", t=4))
+        nc.sync.dma_start(out=s2[:], in_=sign2.rearrange("(p t) n -> p (t n)", t=4))
+        for r in range(3, R):
+            load_x(r)
+
+        ident = const.tile([P, P], F32, name="ident")
+        masks.make_identity(nc, ident[:])
+        warm_in = const.tile([P, 1], F32, name="warm_in")
+        warm_out = const.tile([P, 1], F32, name="warm_out")
+        nc.vector.memset(warm_in[:], 0.0)
+        nc.scalar.activation(out=warm_out[:], in_=warm_in[:], func=ACT.Relu)
+
+        w1g = const.tile([P, 4 * F], BF16, name="w1g", align_bytes=64)
+        w1q = const.tile([P, F], U32, name="w1q", align_bytes=64)
+        w1s = const.tile([P, F], U8, name="w1s", align_bytes=64)
+        w1g_v = w1g[:].rearrange("p (q m t) -> p q m t", q=4, m=P, t=4)
+        t1_v = t1[:].rearrange("p (t m q) -> p q m t", t=4, m=P, q=4)
+        s1_v = s1[:].rearrange("p (t m q) -> p q m t", t=4, m=P, q=4)
+        for q in range(4):
+            nc.vector.scalar_tensor_tensor(
+                out=w1g_v[:, q], in0=t1_v[:, q], scalar=0.0, in1=s1_v[:, q], op0=ALU.max, op1=ALU.mult
+            )
+        nc.vector.quantize_mx(out=w1q[:].bitcast(FP8X4), scales=w1s[:], in_=w1g[:])
+
+        w2g = const.tile([P, 4 * N], BF16, name="w2g", align_bytes=64)
+        w2q = const.tile([P, N], U32, name="w2q", align_bytes=64)
+        w2s = const.tile([P, N], U8, name="w2s", align_bytes=64)
+
+        def w2_mask():
+            nc.vector.scalar_tensor_tensor(
+                out=w2g[:].rearrange("p (n t) -> p n t", t=4),
+                in0=t2[:].rearrange("p (t n) -> p n t", t=4),
+                scalar=0.0,
+                in1=s2[:].rearrange("p (t n) -> p n t", t=4),
+                op0=ALU.max,
+                op1=ALU.mult,
+            )
+
+        def w2_quant():
+            nc.vector.quantize_mx(out=w2q[:].bitcast(FP8X4), scales=w2s[:], in_=w2g[:])
+
+        tp = {}
+        xg = {}
+        xq = {}
+        xc = {}
+        hp = {}
+        hg = {}
+        hq = {}
+        hc = {}
+        op = {}
+
+        def relu_out(eng, dst, src):
+            if eng == "S":
+                nc.scalar.activation(out=dst, in_=src, func=ACT.Relu)
+            else:
+                nc.vector.tensor_scalar_max(out=dst, in0=src, scalar1=0.0)
+
+        def transposes(r, h):
+            bank = tpool.tile([P, 512], F32, name="tp")
+            tp[(r, h)] = bank
+            words = xs[r][:].bitcast(F32)
+            for jl in range(2):
+                for u in range(2):
+                    c = (2 * h + jl) * 256 + u * P
+                    nc.tensor.transpose(bank[:, (2 * jl + u) * P : (2 * jl + u + 1) * P], words[:, c : c + P], ident[:])
+
+        def x_copy(r, h, eng):
+            if h == 0:
+                xg[r] = ring.tile([P, RT * D], BF16, name="xg", align_bytes=64)
+            dst = xg[r][:].bitcast(F32)[:, 512 * h : 512 * (h + 1)].rearrange("p (j r u) -> p j r u", j=2, r=P, u=2)
+            src = tp[(r, h)][:].rearrange("p (j u r) -> p j r u", j=2, u=2, r=P)
+            if eng == "S":
+                nc.scalar.copy(out=dst, in_=src)
+            else:
+                nc.vector.tensor_copy(out=dst, in_=src)
+
+        def x_quant(r):
+            xq[r] = ring.tile([P, RT * P], U32, name="xq", align_bytes=64)
+            xc[r] = ring.tile([P, RT * P], U8, name="xc", align_bytes=64)
+            nc.vector.quantize_mx(out=xq[r][:].bitcast(FP8X4), scales=xc[r][:], in_=xg[r][:])
+
+        def layer1(r, j):
+            bank = hpool.tile([P, 512], F32, name="hp")
+            hp[(r, j)] = bank
+            tok = slice(j * P, (j + 1) * P)
+            for q in range(4):
+                cols = slice(q * P, (q + 1) * P)
+                nc.tensor.matmul_mx(
+                    out=bank[:, cols],
+                    lhsT=w1q[:, cols].bitcast(FP8X4),
+                    lhsT_scale=w1s[:, cols],
+                    rhs=xq[r][:, tok].bitcast(FP8X4),
+                    rhs_scale=xc[r][:, tok],
+                    start=True,
+                    stop=True,
+                )
+
+        def h_copy(r, j, eng):
+            if j == 0:
+                hg[r] = ring.tile([P, RT * F], BF16, name="hg", align_bytes=64)
+            dst = hg[r][:, j * F : (j + 1) * F].rearrange("p (r t) -> p r t", t=4)
+            src = hp[(r, j)][:].rearrange("p (t r) -> p r t", t=4)
+            relu_out(eng, dst, src)
+
+        def h_quant(r):
+            hq[r] = ring.tile([P, RT * P], U32, name="hq", align_bytes=64)
+            hc[r] = ring.tile([P, RT * P], U8, name="hc", align_bytes=64)
+            nc.vector.quantize_mx(out=hq[r][:].bitcast(FP8X4), scales=hc[r][:], in_=hg[r][:])
+
+        def layer2(r, h):
+            bank = opool.tile([P, 512], F32, name="op")
+            op[(r, h)] = bank
+            for jl in range(2):
+                tok = slice((2 * h + jl) * P, (2 * h + jl + 1) * P)
+                nc.tensor.matmul_mx(
+                    out=bank[:, jl * N : (jl + 1) * N],
+                    lhsT=hq[r][:, tok].bitcast(FP8X4),
+                    lhsT_scale=hc[r][:, tok],
+                    rhs=w2q[:].bitcast(FP8X4),
+                    rhs_scale=w2s[:],
+                    start=True,
+                    stop=True,
+                )
+
+        def o_copy(r, h, eng):
+            relu_out(eng, ob[r][:, 512 * h : 512 * (h + 1)], op[(r, h)][:])
+
+        def store(r):
+            nc.sync.dma_start(out=ov[:, r * RT * N : (r + 1) * RT * N], in_=ob[r][:])
+
+        def live(r):
+            return 0 <= r < R
+
+        for s in range(-LEAD, R + 1):
+            if live(s - 1):
+                h_quant(s - 1)
+            if live(s + LEAD - 1):
+                for h in range(2):
+                    x_copy(s + LEAD - 1, h, "S" if s + LEAD - 1 < 2 else "V")
+            if s == 0:
+                w2_mask()
+            if live(s + 1):
+                x_quant(s + 1)
+            if s == 0:
+                w2_quant()
+            if live(s):
+                for j in range(RT):
+                    layer1(s, j)
+                for j in range(RT):
+                    h_copy(s, j, "V" if (s >= R - 2 and j == 1) else "S")
+            if live(s - 1):
+                for h in range(2):
+                    layer2(s - 1, h)
+                o_copy(s - 1, 0, "S")
+                o_copy(s - 1, 1, "V")
+                store(s - 1)
+            if live(s + LEAD):
+                for h in range(2):
+                    transposes(s + LEAD, h)

@@ -19,10 +19,76 @@ N = 256
 TILES = TOKENS // P
 RT = 4
 R = TILES // RT
-LEAD = 3
-MANUAL = True
 
 FLOPS = 2 * TOKENS * D * (F + N)
+
+PLAN = (
+    ("W1G", 0, 0, "V"), ("W1G", 1, 0, "V"), ("T", 0, 0, "PE"), ("W1G", 2, 0, "V"), ("T", 0, 1, "PE"), ("XC", 0, 0, "S"),
+    ("W1G", 3, 0, "V"), ("XC", 0, 1, "S"), ("T", 1, 0, "PE"), ("XQ", 0, 0, "V"), ("W1Q", 0, 0, "V"), ("T", 1, 1, "PE"),
+    ("XC", 1, 0, "S"), ("XQ", 0, 1, "V"), ("XC", 1, 1, "S"), ("T", 2, 0, "PE"), ("T", 2, 1, "PE"), ("XC", 2, 0, "S"),
+    ("L1", 0, 0, "PE"), ("W2G", 0, 0, "V"), ("XC", 2, 1, "S"), ("L1", 0, 1, "PE"), ("L1", 0, 2, "PE"), ("HC", 0, 0, "S"),
+    ("L1", 0, 3, "PE"), ("XQ", 1, 0, "V"), ("T", 3, 0, "PE"), ("HC", 0, 1, "S"), ("T", 3, 1, "PE"), ("W2Q", 0, 0, "V"),
+    ("HC", 0, 2, "S"), ("L1", 1, 0, "PE"), ("XC", 3, 0, "V"), ("HC", 0, 3, "S"), ("L1", 1, 1, "PE"), ("XC", 3, 1, "V"),
+    ("L1", 1, 2, "PE"), ("HC", 1, 0, "S"), ("L1", 1, 3, "PE"), ("XQ", 2, 0, "V"), ("T", 4, 0, "PE"), ("HC", 1, 1, "S"),
+    ("HQ", 0, 0, "V"), ("T", 4, 1, "PE"), ("HC", 1, 2, "S"), ("L1", 2, 0, "PE"), ("XC", 4, 0, "V"), ("HC", 1, 3, "S"),
+    ("L1", 2, 1, "PE"), ("L1", 2, 2, "PE"), ("XC", 4, 1, "V"), ("HC", 2, 0, "S"), ("L1", 2, 3, "PE"), ("XQ", 3, 0, "V"),
+    ("L2", 0, 0, "PE"), ("HC", 2, 1, "S"), ("L2", 0, 1, "PE"), ("T", 5, 0, "PE"), ("HC", 2, 2, "S"), ("OC", 0, 1, "V"),
+    ("T", 5, 1, "PE"), ("HC", 2, 3, "S"), ("L1", 3, 0, "PE"), ("HQ", 1, 0, "V"), ("L1", 3, 1, "PE"), ("OC", 0, 0, "S"),
+    ("XC", 5, 0, "V"), ("L1", 3, 2, "PE"), ("HC", 3, 0, "S"), ("L1", 3, 3, "PE"), ("XC", 5, 1, "V"), ("L2", 1, 0, "PE"),
+    ("HC", 3, 1, "S"), ("L2", 1, 1, "PE"), ("XQ", 4, 0, "V"), ("T", 6, 0, "PE"), ("HC", 3, 2, "S"), ("T", 6, 1, "PE"),
+    ("OC", 1, 1, "V"), ("HC", 3, 3, "S"), ("L1", 4, 0, "PE"), ("HQ", 2, 0, "V"), ("L1", 4, 1, "PE"), ("OC", 1, 0, "S"),
+    ("L1", 4, 2, "PE"), ("XC", 6, 0, "V"), ("L1", 4, 3, "PE"), ("HC", 4, 0, "S"), ("L2", 2, 0, "PE"), ("XC", 6, 1, "V"),
+    ("L2", 2, 1, "PE"), ("HC", 4, 1, "S"), ("T", 7, 0, "PE"), ("XQ", 5, 0, "V"), ("HC", 4, 2, "S"), ("T", 7, 1, "PE"),
+    ("OC", 2, 1, "V"), ("HC", 4, 3, "S"), ("L1", 5, 0, "PE"), ("HQ", 3, 0, "V"), ("L1", 5, 1, "PE"), ("OC", 2, 0, "S"),
+    ("ST", 0, 0, "DMA"), ("L1", 5, 2, "PE"), ("XC", 7, 0, "V"), ("L1", 5, 3, "PE"), ("HC", 5, 0, "S"), ("L2", 3, 0, "PE"),
+    ("XC", 7, 1, "V"), ("HC", 5, 1, "S"), ("L2", 3, 1, "PE"), ("ST", 1, 0, "DMA"), ("T", 8, 0, "PE"), ("XQ", 6, 0, "V"),
+    ("HC", 5, 2, "S"), ("T", 8, 1, "PE"), ("OC", 3, 1, "V"), ("HC", 5, 3, "S"), ("L1", 6, 0, "PE"), ("ST", 2, 0, "DMA"),
+    ("HQ", 4, 0, "V"), ("L1", 6, 1, "PE"), ("OC", 3, 0, "S"), ("L1", 6, 2, "PE"), ("XC", 8, 0, "V"), ("HC", 6, 0, "S"),
+    ("L1", 6, 3, "PE"), ("L2", 4, 0, "PE"), ("XC", 8, 1, "V"), ("ST", 3, 0, "DMA"), ("HC", 6, 1, "S"), ("L2", 4, 1, "PE"),
+    ("T", 9, 0, "PE"), ("XQ", 7, 0, "V"), ("HC", 6, 2, "S"), ("T", 9, 1, "PE"), ("HQ", 5, 0, "V"), ("HC", 6, 3, "S"),
+    ("L1", 7, 0, "PE"), ("XC", 9, 0, "V"), ("OC", 4, 0, "S"), ("L1", 7, 1, "PE"), ("L1", 7, 2, "PE"), ("XC", 9, 1, "V"),
+    ("OC", 4, 1, "S"), ("L1", 7, 3, "PE"), ("L2", 5, 0, "PE"), ("XQ", 8, 0, "V"), ("HC", 7, 0, "S"), ("ST", 4, 0, "DMA"),
+    ("L2", 5, 1, "PE"), ("T", 10, 0, "PE"), ("HC", 7, 1, "S"), ("OC", 5, 1, "V"), ("T", 10, 1, "PE"), ("HC", 7, 2, "S"),
+    ("L1", 8, 0, "PE"), ("HQ", 6, 0, "V"), ("L1", 8, 1, "PE"), ("HC", 7, 3, "S"), ("XC", 10, 0, "V"), ("L1", 8, 2, "PE"),
+    ("OC", 5, 0, "S"), ("L1", 8, 3, "PE"), ("XC", 10, 1, "V"), ("HC", 8, 0, "S"), ("ST", 5, 0, "DMA"), ("L2", 6, 0, "PE"),
+    ("XQ", 9, 0, "V"), ("L2", 6, 1, "PE"), ("HC", 8, 1, "S"), ("T", 11, 0, "PE"), ("OC", 6, 1, "V"), ("T", 11, 1, "PE"),
+    ("HC", 8, 2, "S"), ("L1", 9, 0, "PE"), ("HQ", 7, 0, "V"), ("HC", 8, 3, "S"), ("L1", 9, 1, "PE"), ("XC", 11, 0, "V"),
+    ("L1", 9, 2, "PE"), ("OC", 6, 0, "S"), ("L1", 9, 3, "PE"), ("XC", 11, 1, "V"), ("HC", 9, 0, "S"), ("ST", 6, 0, "DMA"),
+    ("L2", 7, 0, "PE"), ("L2", 7, 1, "PE"), ("XQ", 10, 0, "V"), ("HC", 9, 1, "S"), ("T", 12, 0, "PE"), ("OC", 7, 1, "V"),
+    ("T", 12, 1, "PE"), ("HC", 9, 2, "S"), ("L1", 10, 0, "PE"), ("HQ", 8, 0, "V"), ("HC", 9, 3, "S"), ("L1", 10, 1, "PE"),
+    ("L1", 10, 2, "PE"), ("XC", 12, 0, "V"), ("OC", 7, 0, "S"), ("L1", 10, 3, "PE"), ("XC", 12, 1, "V"), ("HC", 10, 0, "S"),
+    ("ST", 7, 0, "DMA"), ("L2", 8, 0, "PE"), ("L2", 8, 1, "PE"), ("XQ", 11, 0, "V"), ("HC", 10, 1, "S"), ("T", 13, 0, "PE"),
+    ("T", 13, 1, "PE"), ("HC", 10, 2, "S"), ("OC", 8, 1, "V"), ("L1", 11, 0, "PE"), ("HC", 10, 3, "S"), ("HQ", 9, 0, "V"),
+    ("L1", 11, 1, "PE"), ("L1", 11, 2, "PE"), ("OC", 8, 0, "S"), ("XC", 13, 0, "V"), ("L1", 11, 3, "PE"), ("HC", 11, 0, "S"),
+    ("XC", 13, 1, "V"), ("ST", 8, 0, "DMA"), ("L2", 9, 0, "PE"), ("L2", 9, 1, "PE"), ("HC", 11, 1, "S"), ("XQ", 12, 0, "V"),
+    ("T", 14, 0, "PE"), ("T", 14, 1, "PE"), ("HC", 11, 2, "S"), ("OC", 9, 1, "V"), ("L1", 12, 0, "PE"), ("HC", 11, 3, "S"),
+    ("HQ", 10, 0, "V"), ("L1", 12, 1, "PE"), ("L1", 12, 2, "PE"), ("OC", 9, 0, "S"), ("XC", 14, 1, "V"), ("L1", 12, 3, "PE"),
+    ("XC", 14, 0, "S"), ("ST", 9, 0, "DMA"), ("L2", 10, 0, "PE"), ("XQ", 13, 0, "V"), ("L2", 10, 1, "PE"), ("HC", 12, 0, "S"),
+    ("T", 15, 0, "PE"), ("OC", 10, 1, "V"), ("T", 15, 1, "PE"), ("HC", 12, 1, "S"), ("L1", 13, 0, "PE"), ("HQ", 11, 0, "V"),
+    ("HC", 12, 2, "S"), ("L1", 13, 1, "PE"), ("XC", 15, 0, "V"), ("HC", 12, 3, "S"), ("L1", 13, 2, "PE"), ("XC", 15, 1, "V"),
+    ("OC", 10, 0, "S"), ("L1", 13, 3, "PE"), ("XQ", 14, 0, "V"), ("HC", 13, 0, "S"), ("ST", 10, 0, "DMA"), ("L2", 11, 0, "PE"),
+    ("L2", 11, 1, "PE"), ("HC", 13, 1, "V"), ("HC", 13, 2, "S"), ("L1", 14, 0, "PE"), ("OC", 11, 1, "V"), ("HC", 13, 3, "S"),
+    ("L1", 14, 1, "PE"), ("L1", 14, 2, "PE"), ("HQ", 12, 0, "V"), ("OC", 11, 0, "S"), ("L1", 14, 3, "PE"), ("XQ", 15, 0, "V"),
+    ("HC", 14, 0, "S"), ("ST", 11, 0, "DMA"), ("L2", 12, 0, "PE"), ("L2", 12, 1, "PE"), ("HC", 14, 1, "V"), ("HC", 14, 3, "S"),
+    ("L1", 15, 0, "PE"), ("OC", 12, 0, "S"), ("HC", 14, 2, "V"), ("L1", 15, 1, "PE"), ("OC", 12, 1, "S"), ("HQ", 13, 0, "V"),
+    ("L1", 15, 2, "PE"), ("L1", 15, 3, "PE"), ("HC", 15, 0, "V"), ("ST", 12, 0, "DMA"), ("HC", 15, 2, "S"), ("L2", 13, 0, "PE"),
+    ("L2", 13, 1, "PE"), ("HC", 15, 1, "V"), ("HC", 15, 3, "S"), ("HQ", 14, 0, "V"), ("OC", 13, 0, "S"), ("HQ", 14, 1, "V"),
+    ("HQ", 15, 0, "V"), ("OC", 13, 1, "S"), ("ST", 13, 0, "DMA"), ("L2", 14, 0, "PE"), ("HQ", 15, 1, "V"), ("L2", 14, 1, "PE"),
+    ("OC", 14, 0, "S"), ("ST", 13, 1, "DMA"), ("OC", 14, 1, "S"), ("ST", 14, 0, "DMA"), ("L2", 15, 0, "PE"), ("L2", 15, 1, "PE"),
+    ("OC", 15, 0, "S"), ("ST", 14, 1, "DMA"), ("OC", 15, 1, "V"), ("ST", 15, 0, "DMA"), ("ST", 15, 1, "DMA"),
+)
+
+
+def x_parts(r):
+    return 2 if r == 0 else 1
+
+
+def h_parts(r):
+    return 2 if r >= 14 else 1
+
+
+def s_parts(r):
+    return 2 if r >= 13 else 1
 
 
 def tile_sparse_connect_t_kernel(tc, x, th1, sign1, th2, sign2, relu, out):
@@ -32,10 +98,10 @@ def tile_sparse_connect_t_kernel(tc, x, th1, sign1, th2, sign2, relu, out):
     ov = out.flatten_outer_dims().rearrange("(p j) n -> p (j n)", j=TILES)
 
     with ExitStack() as ctx:
-        if MANUAL:
-            ctx.enter_context(tc.manual_schedule())
+        ctx.enter_context(tc.manual_schedule())
         const = ctx.enter_context(tc.tile_pool(name="const", bufs=1))
-        ring = ctx.enter_context(tc.tile_pool(name="ring", bufs=3))
+        ring4 = ctx.enter_context(tc.tile_pool(name="ring4", bufs=4))
+        ring5 = ctx.enter_context(tc.tile_pool(name="ring5", bufs=5))
         tpool = ctx.enter_context(tc.psum_pool(name="tpool", bufs=2))
         hpool = ctx.enter_context(tc.psum_pool(name="hpool", bufs=4))
         opool = ctx.enter_context(tc.psum_pool(name="opool", bufs=2))
@@ -78,15 +144,17 @@ def tile_sparse_connect_t_kernel(tc, x, th1, sign1, th2, sign2, relu, out):
         w1g_v = w1g[:].rearrange("p (q m t) -> p q m t", q=4, m=P, t=4)
         t1_v = t1[:].rearrange("p (t m q) -> p q m t", t=4, m=P, q=4)
         s1_v = s1[:].rearrange("p (t m q) -> p q m t", t=4, m=P, q=4)
-        for q in range(4):
-            nc.vector.scalar_tensor_tensor(
-                out=w1g_v[:, q], in0=t1_v[:, q], scalar=0.0, in1=s1_v[:, q], op0=ALU.max, op1=ALU.mult
-            )
-        nc.vector.quantize_mx(out=w1q[:].bitcast(FP8X4), scales=w1s[:], in_=w1g[:])
-
         w2g = const.tile([P, 4 * N], BF16, name="w2g", align_bytes=64)
         w2q = const.tile([P, N], U32, name="w2q", align_bytes=64)
         w2s = const.tile([P, N], U8, name="w2s", align_bytes=64)
+
+        def w1_mask(q):
+            nc.vector.scalar_tensor_tensor(
+                out=w1g_v[:, q], in0=t1_v[:, q], scalar=0.0, in1=s1_v[:, q], op0=ALU.max, op1=ALU.mult
+            )
+
+        def w1_quant():
+            nc.vector.quantize_mx(out=w1q[:].bitcast(FP8X4), scales=w1s[:], in_=w1g[:])
 
         def w2_mask():
             nc.vector.scalar_tensor_tensor(
@@ -127,8 +195,8 @@ def tile_sparse_connect_t_kernel(tc, x, th1, sign1, th2, sign2, relu, out):
                     nc.tensor.transpose(bank[:, (2 * jl + u) * P : (2 * jl + u + 1) * P], words[:, c : c + P], ident[:])
 
         def x_copy(r, h, eng):
-            if h == 0:
-                xg[r] = ring.tile([P, RT * D], BF16, name="xg", align_bytes=64)
+            if r not in xg:
+                xg[r] = ring4.tile([P, RT * D], BF16, name="xg", align_bytes=64)
             dst = xg[r][:].bitcast(F32)[:, 512 * h : 512 * (h + 1)].rearrange("p (j r u) -> p j r u", j=2, r=P, u=2)
             src = tp[(r, h)][:].rearrange("p (j u r) -> p j r u", j=2, u=2, r=P)
             if eng == "S":
@@ -136,10 +204,19 @@ def tile_sparse_connect_t_kernel(tc, x, th1, sign1, th2, sign2, relu, out):
             else:
                 nc.vector.tensor_copy(out=dst, in_=src)
 
-        def x_quant(r):
-            xq[r] = ring.tile([P, RT * P], U32, name="xq", align_bytes=64)
-            xc[r] = ring.tile([P, RT * P], U8, name="xc", align_bytes=64)
-            nc.vector.quantize_mx(out=xq[r][:].bitcast(FP8X4), scales=xc[r][:], in_=xg[r][:])
+        def quant(words, plane, values, k, parts):
+            w = RT * P // parts
+            nc.vector.quantize_mx(
+                out=words[:, k * w : (k + 1) * w].bitcast(FP8X4),
+                scales=plane[:, k * w : (k + 1) * w],
+                in_=values[:, 4 * k * w : 4 * (k + 1) * w],
+            )
+
+        def x_quant(r, k):
+            if r not in xq:
+                xq[r] = ring5.tile([P, RT * P], U32, name="xq", align_bytes=64)
+                xc[r] = ring5.tile([P, RT * P], U8, name="xc", align_bytes=64)
+            quant(xq[r], xc[r], xg[r], k, x_parts(r))
 
         def layer1(r, j):
             bank = hpool.tile([P, 512], F32, name="hp")
@@ -158,16 +235,17 @@ def tile_sparse_connect_t_kernel(tc, x, th1, sign1, th2, sign2, relu, out):
                 )
 
         def h_copy(r, j, eng):
-            if j == 0:
-                hg[r] = ring.tile([P, RT * F], BF16, name="hg", align_bytes=64)
+            if r not in hg:
+                hg[r] = ring4.tile([P, RT * F], BF16, name="hg", align_bytes=64)
             dst = hg[r][:, j * F : (j + 1) * F].rearrange("p (r t) -> p r t", t=4)
             src = hp[(r, j)][:].rearrange("p (t r) -> p r t", t=4)
             relu_out(eng, dst, src)
 
-        def h_quant(r):
-            hq[r] = ring.tile([P, RT * P], U32, name="hq", align_bytes=64)
-            hc[r] = ring.tile([P, RT * P], U8, name="hc", align_bytes=64)
-            nc.vector.quantize_mx(out=hq[r][:].bitcast(FP8X4), scales=hc[r][:], in_=hg[r][:])
+        def h_quant(r, k):
+            if r not in hq:
+                hq[r] = ring4.tile([P, RT * P], U32, name="hq", align_bytes=64)
+                hc[r] = ring4.tile([P, RT * P], U8, name="hc", align_bytes=64)
+            quant(hq[r], hc[r], hg[r], k, h_parts(r))
 
         def layer2(r, h):
             bank = opool.tile([P, 512], F32, name="op")
@@ -187,35 +265,34 @@ def tile_sparse_connect_t_kernel(tc, x, th1, sign1, th2, sign2, relu, out):
         def o_copy(r, h, eng):
             relu_out(eng, ob[r][:, 512 * h : 512 * (h + 1)], op[(r, h)][:])
 
-        def store(r):
-            nc.sync.dma_start(out=ov[:, r * RT * N : (r + 1) * RT * N], in_=ob[r][:])
+        def store(r, k):
+            w = RT * N // s_parts(r)
+            nc.sync.dma_start(out=ov[:, r * RT * N + k * w : r * RT * N + (k + 1) * w], in_=ob[r][:, k * w : (k + 1) * w])
 
-        def live(r):
-            return 0 <= r < R
-
-        for s in range(-LEAD, R + 1):
-            if live(s - 1):
-                h_quant(s - 1)
-            if live(s + LEAD - 1):
-                for h in range(2):
-                    x_copy(s + LEAD - 1, h, "S" if s + LEAD - 1 < 2 else "V")
-            if s == 0:
+        for what, r, i, eng in PLAN:
+            if what == "W1G":
+                w1_mask(r)
+            elif what == "W1Q":
+                w1_quant()
+            elif what == "W2G":
                 w2_mask()
-            if live(s + 1):
-                x_quant(s + 1)
-            if s == 0:
+            elif what == "W2Q":
                 w2_quant()
-            if live(s):
-                for j in range(RT):
-                    layer1(s, j)
-                for j in range(RT):
-                    h_copy(s, j, "V" if (s >= R - 2 and j == 1) else "S")
-            if live(s - 1):
-                for h in range(2):
-                    layer2(s - 1, h)
-                o_copy(s - 1, 0, "S")
-                o_copy(s - 1, 1, "V")
-                store(s - 1)
-            if live(s + LEAD):
-                for h in range(2):
-                    transposes(s + LEAD, h)
+            elif what == "T":
+                transposes(r, i)
+            elif what == "XC":
+                x_copy(r, i, eng)
+            elif what == "XQ":
+                x_quant(r, i)
+            elif what == "L1":
+                layer1(r, i)
+            elif what == "HC":
+                h_copy(r, i, eng)
+            elif what == "HQ":
+                h_quant(r, i)
+            elif what == "L2":
+                layer2(r, i)
+            elif what == "OC":
+                o_copy(r, i, eng)
+            else:
+                store(r, i)

@@ -12,106 +12,67 @@ ALU = mybir.AluOpType
 ACT = mybir.ActivationFunctionType
 
 P = 128
+PACK = 4
 TOKENS = 8192
 D = 512
 F = 512
 N = 256
+BANK = 512
 TILES = TOKENS // P
-RT = 4
-R = TILES // RT
+ROUND = 4
+ROUNDS = TILES // ROUND
+AHEAD = 3
+BEHIND = 2
 
 FLOPS = 2 * TOKENS * D * (F + N)
 
-PLAN = (
-    ("W1G", 0, 0, "V"), ("W1G", 1, 0, "V"), ("T", 0, 0, "PE"), ("W1G", 2, 0, "V"), ("T", 0, 1, "PE"), ("XC", 0, 0, "S"),
-    ("W1G", 3, 0, "V"), ("XC", 0, 1, "S"), ("T", 1, 0, "PE"), ("XQ", 0, 0, "V"), ("W1Q", 0, 0, "V"), ("T", 1, 1, "PE"),
-    ("XC", 1, 0, "S"), ("XQ", 0, 1, "V"), ("XC", 1, 1, "S"), ("T", 2, 0, "PE"), ("T", 2, 1, "PE"), ("XC", 2, 0, "S"),
-    ("L1", 0, 0, "PE"), ("W2G", 0, 0, "V"), ("XC", 2, 1, "S"), ("L1", 0, 1, "PE"), ("L1", 0, 2, "PE"), ("HC", 0, 0, "S"),
-    ("L1", 0, 3, "PE"), ("XQ", 1, 0, "V"), ("T", 3, 0, "PE"), ("HC", 0, 1, "S"), ("T", 3, 1, "PE"), ("W2Q", 0, 0, "V"),
-    ("HC", 0, 2, "S"), ("L1", 1, 0, "PE"), ("XC", 3, 0, "V"), ("HC", 0, 3, "S"), ("L1", 1, 1, "PE"), ("XC", 3, 1, "V"),
-    ("L1", 1, 2, "PE"), ("HC", 1, 0, "S"), ("L1", 1, 3, "PE"), ("XQ", 2, 0, "V"), ("T", 4, 0, "PE"), ("HC", 1, 1, "S"),
-    ("HQ", 0, 0, "V"), ("T", 4, 1, "PE"), ("HC", 1, 2, "S"), ("L1", 2, 0, "PE"), ("XC", 4, 0, "V"), ("HC", 1, 3, "S"),
-    ("L1", 2, 1, "PE"), ("L1", 2, 2, "PE"), ("XC", 4, 1, "V"), ("HC", 2, 0, "S"), ("L1", 2, 3, "PE"), ("XQ", 3, 0, "V"),
-    ("L2", 0, 0, "PE"), ("HC", 2, 1, "S"), ("L2", 0, 1, "PE"), ("T", 5, 0, "PE"), ("HC", 2, 2, "S"), ("OC", 0, 1, "V"),
-    ("T", 5, 1, "PE"), ("HC", 2, 3, "S"), ("L1", 3, 0, "PE"), ("HQ", 1, 0, "V"), ("L1", 3, 1, "PE"), ("OC", 0, 0, "S"),
-    ("XC", 5, 0, "V"), ("L1", 3, 2, "PE"), ("HC", 3, 0, "S"), ("L1", 3, 3, "PE"), ("XC", 5, 1, "V"), ("L2", 1, 0, "PE"),
-    ("HC", 3, 1, "S"), ("L2", 1, 1, "PE"), ("XQ", 4, 0, "V"), ("T", 6, 0, "PE"), ("HC", 3, 2, "S"), ("T", 6, 1, "PE"),
-    ("OC", 1, 1, "V"), ("HC", 3, 3, "S"), ("L1", 4, 0, "PE"), ("HQ", 2, 0, "V"), ("L1", 4, 1, "PE"), ("OC", 1, 0, "S"),
-    ("L1", 4, 2, "PE"), ("XC", 6, 0, "V"), ("L1", 4, 3, "PE"), ("HC", 4, 0, "S"), ("L2", 2, 0, "PE"), ("XC", 6, 1, "V"),
-    ("L2", 2, 1, "PE"), ("HC", 4, 1, "S"), ("T", 7, 0, "PE"), ("XQ", 5, 0, "V"), ("HC", 4, 2, "S"), ("T", 7, 1, "PE"),
-    ("OC", 2, 1, "V"), ("HC", 4, 3, "S"), ("L1", 5, 0, "PE"), ("HQ", 3, 0, "V"), ("L1", 5, 1, "PE"), ("OC", 2, 0, "S"),
-    ("ST", 0, 0, "DMA"), ("L1", 5, 2, "PE"), ("XC", 7, 0, "V"), ("L1", 5, 3, "PE"), ("HC", 5, 0, "S"), ("L2", 3, 0, "PE"),
-    ("XC", 7, 1, "V"), ("HC", 5, 1, "S"), ("L2", 3, 1, "PE"), ("ST", 1, 0, "DMA"), ("T", 8, 0, "PE"), ("XQ", 6, 0, "V"),
-    ("HC", 5, 2, "S"), ("T", 8, 1, "PE"), ("OC", 3, 1, "V"), ("HC", 5, 3, "S"), ("L1", 6, 0, "PE"), ("ST", 2, 0, "DMA"),
-    ("HQ", 4, 0, "V"), ("L1", 6, 1, "PE"), ("OC", 3, 0, "S"), ("L1", 6, 2, "PE"), ("XC", 8, 0, "V"), ("HC", 6, 0, "S"),
-    ("L1", 6, 3, "PE"), ("L2", 4, 0, "PE"), ("XC", 8, 1, "V"), ("ST", 3, 0, "DMA"), ("HC", 6, 1, "S"), ("L2", 4, 1, "PE"),
-    ("T", 9, 0, "PE"), ("XQ", 7, 0, "V"), ("HC", 6, 2, "S"), ("T", 9, 1, "PE"), ("HQ", 5, 0, "V"), ("HC", 6, 3, "S"),
-    ("L1", 7, 0, "PE"), ("XC", 9, 0, "V"), ("OC", 4, 0, "S"), ("L1", 7, 1, "PE"), ("L1", 7, 2, "PE"), ("XC", 9, 1, "V"),
-    ("OC", 4, 1, "S"), ("L1", 7, 3, "PE"), ("L2", 5, 0, "PE"), ("XQ", 8, 0, "V"), ("HC", 7, 0, "S"), ("ST", 4, 0, "DMA"),
-    ("L2", 5, 1, "PE"), ("T", 10, 0, "PE"), ("HC", 7, 1, "S"), ("OC", 5, 1, "V"), ("T", 10, 1, "PE"), ("HC", 7, 2, "S"),
-    ("L1", 8, 0, "PE"), ("HQ", 6, 0, "V"), ("L1", 8, 1, "PE"), ("HC", 7, 3, "S"), ("XC", 10, 0, "V"), ("L1", 8, 2, "PE"),
-    ("OC", 5, 0, "S"), ("L1", 8, 3, "PE"), ("XC", 10, 1, "V"), ("HC", 8, 0, "S"), ("ST", 5, 0, "DMA"), ("L2", 6, 0, "PE"),
-    ("XQ", 9, 0, "V"), ("L2", 6, 1, "PE"), ("HC", 8, 1, "S"), ("T", 11, 0, "PE"), ("OC", 6, 1, "V"), ("T", 11, 1, "PE"),
-    ("HC", 8, 2, "S"), ("L1", 9, 0, "PE"), ("HQ", 7, 0, "V"), ("HC", 8, 3, "S"), ("L1", 9, 1, "PE"), ("XC", 11, 0, "V"),
-    ("L1", 9, 2, "PE"), ("OC", 6, 0, "S"), ("L1", 9, 3, "PE"), ("XC", 11, 1, "V"), ("HC", 9, 0, "S"), ("ST", 6, 0, "DMA"),
-    ("L2", 7, 0, "PE"), ("L2", 7, 1, "PE"), ("XQ", 10, 0, "V"), ("HC", 9, 1, "S"), ("T", 12, 0, "PE"), ("OC", 7, 1, "V"),
-    ("T", 12, 1, "PE"), ("HC", 9, 2, "S"), ("L1", 10, 0, "PE"), ("HQ", 8, 0, "V"), ("HC", 9, 3, "S"), ("L1", 10, 1, "PE"),
-    ("L1", 10, 2, "PE"), ("XC", 12, 0, "V"), ("OC", 7, 0, "S"), ("L1", 10, 3, "PE"), ("XC", 12, 1, "V"), ("HC", 10, 0, "S"),
-    ("ST", 7, 0, "DMA"), ("L2", 8, 0, "PE"), ("L2", 8, 1, "PE"), ("XQ", 11, 0, "V"), ("HC", 10, 1, "S"), ("T", 13, 0, "PE"),
-    ("T", 13, 1, "PE"), ("HC", 10, 2, "S"), ("OC", 8, 1, "V"), ("L1", 11, 0, "PE"), ("HC", 10, 3, "S"), ("HQ", 9, 0, "V"),
-    ("L1", 11, 1, "PE"), ("L1", 11, 2, "PE"), ("OC", 8, 0, "S"), ("XC", 13, 0, "V"), ("L1", 11, 3, "PE"), ("HC", 11, 0, "S"),
-    ("XC", 13, 1, "V"), ("ST", 8, 0, "DMA"), ("L2", 9, 0, "PE"), ("L2", 9, 1, "PE"), ("HC", 11, 1, "S"), ("XQ", 12, 0, "V"),
-    ("T", 14, 0, "PE"), ("T", 14, 1, "PE"), ("HC", 11, 2, "S"), ("OC", 9, 1, "V"), ("L1", 12, 0, "PE"), ("HC", 11, 3, "S"),
-    ("HQ", 10, 0, "V"), ("L1", 12, 1, "PE"), ("L1", 12, 2, "PE"), ("OC", 9, 0, "S"), ("XC", 14, 1, "V"), ("L1", 12, 3, "PE"),
-    ("XC", 14, 0, "S"), ("ST", 9, 0, "DMA"), ("L2", 10, 0, "PE"), ("XQ", 13, 0, "V"), ("L2", 10, 1, "PE"), ("HC", 12, 0, "S"),
-    ("T", 15, 0, "PE"), ("OC", 10, 1, "V"), ("T", 15, 1, "PE"), ("HC", 12, 1, "S"), ("L1", 13, 0, "PE"), ("HQ", 11, 0, "V"),
-    ("HC", 12, 2, "S"), ("L1", 13, 1, "PE"), ("XC", 15, 0, "V"), ("HC", 12, 3, "S"), ("L1", 13, 2, "PE"), ("XC", 15, 1, "V"),
-    ("OC", 10, 0, "S"), ("L1", 13, 3, "PE"), ("XQ", 14, 0, "V"), ("HC", 13, 0, "S"), ("ST", 10, 0, "DMA"), ("L2", 11, 0, "PE"),
-    ("L2", 11, 1, "PE"), ("HC", 13, 1, "V"), ("HC", 13, 2, "S"), ("L1", 14, 0, "PE"), ("OC", 11, 1, "V"), ("HC", 13, 3, "S"),
-    ("L1", 14, 1, "PE"), ("L1", 14, 2, "PE"), ("HQ", 12, 0, "V"), ("OC", 11, 0, "S"), ("L1", 14, 3, "PE"), ("XQ", 15, 0, "V"),
-    ("HC", 14, 0, "S"), ("ST", 11, 0, "DMA"), ("L2", 12, 0, "PE"), ("L2", 12, 1, "PE"), ("HC", 14, 1, "V"), ("HC", 14, 3, "S"),
-    ("L1", 15, 0, "PE"), ("OC", 12, 0, "S"), ("HC", 14, 2, "V"), ("L1", 15, 1, "PE"), ("OC", 12, 1, "S"), ("HQ", 13, 0, "V"),
-    ("L1", 15, 2, "PE"), ("L1", 15, 3, "PE"), ("HC", 15, 0, "V"), ("ST", 12, 0, "DMA"), ("HC", 15, 2, "S"), ("L2", 13, 0, "PE"),
-    ("L2", 13, 1, "PE"), ("HC", 15, 1, "V"), ("HC", 15, 3, "S"), ("HQ", 14, 0, "V"), ("OC", 13, 0, "S"), ("HQ", 14, 1, "V"),
-    ("HQ", 15, 0, "V"), ("OC", 13, 1, "S"), ("ST", 13, 0, "DMA"), ("L2", 14, 0, "PE"), ("HQ", 15, 1, "V"), ("L2", 14, 1, "PE"),
-    ("OC", 14, 0, "S"), ("ST", 13, 1, "DMA"), ("OC", 14, 1, "S"), ("ST", 14, 0, "DMA"), ("L2", 15, 0, "PE"), ("L2", 15, 1, "PE"),
-    ("OC", 15, 0, "S"), ("ST", 14, 1, "DMA"), ("OC", 15, 1, "V"), ("ST", 15, 0, "DMA"), ("ST", 15, 1, "DMA"),
-)
+
+def x_copy_engine(r):
+    return "scalar" if r < AHEAD else "vector"
 
 
-def x_parts(r):
+def h_copy_engine(r, j):
+    return "vector" if (r, j) in ((ROUNDS - 2, 1), (ROUNDS - 2, 2), (ROUNDS - 1, 0), (ROUNDS - 1, 1)) else "scalar"
+
+
+def out_copy_engine(r, half):
+    if half == 0 or r in (4, ROUNDS - 4, ROUNDS - 3, ROUNDS - 2):
+        return "scalar"
+    return "vector"
+
+
+def x_quantise_parts(r):
     return 2 if r == 0 else 1
 
 
-def h_parts(r):
-    return 2 if r >= 14 else 1
+def h_quantise_parts(r):
+    return 2 if r >= ROUNDS - 2 else 1
 
 
-def s_parts(r):
-    return 2 if r >= 13 else 1
+def store_parts(r):
+    return 2 if r >= ROUNDS - 3 else 1
 
 
 def tile_sparse_connect_t_kernel(tc, x, th1, sign1, th2, sign2, relu, out):
     assert relu == 1
     nc = tc.nc
-    xv = x.flatten_outer_dims().rearrange("(p j) k -> p (j k)", j=TILES)
-    ov = out.flatten_outer_dims().rearrange("(p j) n -> p (j n)", j=TILES)
+    x_rows = x.flatten_outer_dims().rearrange("(p j) k -> p (j k)", j=TILES)
+    out_rows = out.flatten_outer_dims().rearrange("(p j) n -> p (j n)", j=TILES)
 
     with ExitStack() as ctx:
         ctx.enter_context(tc.manual_schedule())
-        const = ctx.enter_context(tc.tile_pool(name="const", bufs=1))
-        ring4 = ctx.enter_context(tc.tile_pool(name="ring4", bufs=4))
-        ring5 = ctx.enter_context(tc.tile_pool(name="ring5", bufs=5))
-        tpool = ctx.enter_context(tc.psum_pool(name="tpool", bufs=2))
-        hpool = ctx.enter_context(tc.psum_pool(name="hpool", bufs=4))
-        opool = ctx.enter_context(tc.psum_pool(name="opool", bufs=2))
+        keep = ctx.enter_context(tc.tile_pool(name="keep", bufs=1))
+        ring = ctx.enter_context(tc.tile_pool(name="ring", bufs=4))
+        x_banks = ctx.enter_context(tc.psum_pool(name="x_banks", bufs=2))
+        h_banks = ctx.enter_context(tc.psum_pool(name="h_banks", bufs=4))
+        out_banks = ctx.enter_context(tc.psum_pool(name="out_banks", bufs=2))
 
-        t1 = const.tile([P, 4 * F], BF16, name="t1")
-        s1 = const.tile([P, 4 * F], BF16, name="s1")
-        t2 = const.tile([P, 4 * N], BF16, name="t2")
-        s2 = const.tile([P, 4 * N], BF16, name="s2")
-        xs = [const.tile([P, RT * D], BF16, name="xs%d" % r) for r in range(R)]
-        ob = [const.tile([P, RT * N], F32, name="ob%d" % r) for r in range(R)]
+        th1_sb = keep.tile([P, PACK * F], BF16, name="th1_sb")
+        sign1_sb = keep.tile([P, PACK * F], BF16, name="sign1_sb")
+        th2_sb = keep.tile([P, PACK * N], BF16, name="th2_sb")
+        sign2_sb = keep.tile([P, PACK * N], BF16, name="sign2_sb")
+        x_sb = [keep.tile([P, ROUND * D], BF16, name="x_sb%d" % r) for r in range(ROUNDS)]
+        out_sb = [keep.tile([P, ROUND * N], F32, name="out_sb%d" % r) for r in range(ROUNDS)]
 
         def load_w1(dst, src):
             nc.sync.dma_start(
@@ -119,180 +80,202 @@ def tile_sparse_connect_t_kernel(tc, x, th1, sign1, th2, sign2, relu, out):
                 in_=src.rearrange("(u p e) f -> p u (e f)", u=2, p=P, e=2),
             )
 
+        def load_w2(dst, src):
+            nc.sync.dma_start(out=dst[:], in_=src.rearrange("(p t) n -> p (t n)", t=PACK))
+
         def load_x(r):
-            nc.sync.dma_start(out=xs[r][:], in_=xv[:, r * RT * D : (r + 1) * RT * D])
+            nc.sync.dma_start(out=x_sb[r][:], in_=x_rows[:, r * ROUND * D : (r + 1) * ROUND * D])
 
-        load_w1(t1, th1)
-        load_w1(s1, sign1)
-        for r in range(3):
+        load_w1(th1_sb, th1)
+        load_w1(sign1_sb, sign1)
+        for r in range(AHEAD):
             load_x(r)
-        nc.sync.dma_start(out=t2[:], in_=th2.rearrange("(p t) n -> p (t n)", t=4))
-        nc.sync.dma_start(out=s2[:], in_=sign2.rearrange("(p t) n -> p (t n)", t=4))
-        for r in range(3, R):
+        load_w2(th2_sb, th2)
+        load_w2(sign2_sb, sign2)
+        for r in range(AHEAD, ROUNDS):
             load_x(r)
 
-        ident = const.tile([P, P], F32, name="ident")
-        masks.make_identity(nc, ident[:])
-        warm_in = const.tile([P, 1], F32, name="warm_in")
-        warm_out = const.tile([P, 1], F32, name="warm_out")
+        identity = keep.tile([P, P], F32, name="identity")
+        masks.make_identity(nc, identity[:])
+        warm_in = keep.tile([P, 1], F32, name="warm_in")
+        warm_out = keep.tile([P, 1], F32, name="warm_out")
         nc.vector.memset(warm_in[:], 0.0)
         nc.scalar.activation(out=warm_out[:], in_=warm_in[:], func=ACT.Relu)
 
-        w1g = const.tile([P, 4 * F], BF16, name="w1g", align_bytes=64)
-        w1q = const.tile([P, F], U32, name="w1q", align_bytes=64)
-        w1s = const.tile([P, F], U8, name="w1s", align_bytes=64)
-        w1g_v = w1g[:].rearrange("p (q m t) -> p q m t", q=4, m=P, t=4)
-        t1_v = t1[:].rearrange("p (t m q) -> p q m t", t=4, m=P, q=4)
-        s1_v = s1[:].rearrange("p (t m q) -> p q m t", t=4, m=P, q=4)
-        w2g = const.tile([P, 4 * N], BF16, name="w2g", align_bytes=64)
-        w2q = const.tile([P, N], U32, name="w2q", align_bytes=64)
-        w2s = const.tile([P, N], U8, name="w2s", align_bytes=64)
+        w1_values = keep.tile([P, PACK * F], BF16, name="w1_values", align_bytes=64)
+        w1_words = keep.tile([P, F], U32, name="w1_words", align_bytes=64)
+        w1_scales = keep.tile([P, F], U8, name="w1_scales", align_bytes=64)
+        w2_values = keep.tile([P, PACK * N], BF16, name="w2_values", align_bytes=64)
+        w2_words = keep.tile([P, N], U32, name="w2_words", align_bytes=64)
+        w2_scales = keep.tile([P, N], U8, name="w2_scales", align_bytes=64)
 
-        def w1_mask(q):
+        def mask_w1_quarter(q):
             nc.vector.scalar_tensor_tensor(
-                out=w1g_v[:, q], in0=t1_v[:, q], scalar=0.0, in1=s1_v[:, q], op0=ALU.max, op1=ALU.mult
-            )
-
-        def w1_quant():
-            nc.vector.quantize_mx(out=w1q[:].bitcast(FP8X4), scales=w1s[:], in_=w1g[:])
-
-        def w2_mask():
-            nc.vector.scalar_tensor_tensor(
-                out=w2g[:].rearrange("p (n t) -> p n t", t=4),
-                in0=t2[:].rearrange("p (t n) -> p n t", t=4),
+                out=w1_values[:].rearrange("p (q m t) -> p q m t", q=4, m=P, t=PACK)[:, q],
+                in0=th1_sb[:].rearrange("p (t m q) -> p q m t", t=PACK, m=P, q=4)[:, q],
                 scalar=0.0,
-                in1=s2[:].rearrange("p (t n) -> p n t", t=4),
+                in1=sign1_sb[:].rearrange("p (t m q) -> p q m t", t=PACK, m=P, q=4)[:, q],
                 op0=ALU.max,
                 op1=ALU.mult,
             )
 
-        def w2_quant():
-            nc.vector.quantize_mx(out=w2q[:].bitcast(FP8X4), scales=w2s[:], in_=w2g[:])
+        def quantise_w1():
+            nc.vector.quantize_mx(out=w1_words[:].bitcast(FP8X4), scales=w1_scales[:], in_=w1_values[:])
 
-        tp = {}
-        xg = {}
-        xq = {}
-        xc = {}
-        hp = {}
-        hg = {}
-        hq = {}
-        hc = {}
-        op = {}
+        def mask_w2():
+            nc.vector.scalar_tensor_tensor(
+                out=w2_values[:].rearrange("p (n t) -> p n t", t=PACK),
+                in0=th2_sb[:].rearrange("p (t n) -> p n t", t=PACK),
+                scalar=0.0,
+                in1=sign2_sb[:].rearrange("p (t n) -> p n t", t=PACK),
+                op0=ALU.max,
+                op1=ALU.mult,
+            )
 
-        def relu_out(eng, dst, src):
-            if eng == "S":
+        def quantise_w2():
+            nc.vector.quantize_mx(out=w2_words[:].bitcast(FP8X4), scales=w2_scales[:], in_=w2_values[:])
+
+        x_bank = {}
+        x_values = {}
+        x_words = {}
+        x_scales = {}
+        h_bank = {}
+        h_values = {}
+        h_words = {}
+        h_scales = {}
+        out_bank = {}
+
+        def relu_out_of_psum(engine, dst, src):
+            if engine == "scalar":
                 nc.scalar.activation(out=dst, in_=src, func=ACT.Relu)
             else:
                 nc.vector.tensor_scalar_max(out=dst, in0=src, scalar1=0.0)
 
-        def transposes(r, h):
-            bank = tpool.tile([P, 512], F32, name="tp")
-            tp[(r, h)] = bank
-            words = xs[r][:].bitcast(F32)
-            for jl in range(2):
-                for u in range(2):
-                    c = (2 * h + jl) * 256 + u * P
-                    nc.tensor.transpose(bank[:, (2 * jl + u) * P : (2 * jl + u + 1) * P], words[:, c : c + P], ident[:])
+        def quantise_part(words, scales, values, part, parts):
+            w = ROUND * P // parts
+            nc.vector.quantize_mx(
+                out=words[:, part * w : (part + 1) * w].bitcast(FP8X4),
+                scales=scales[:, part * w : (part + 1) * w],
+                in_=values[:, PACK * part * w : PACK * (part + 1) * w],
+            )
 
-        def x_copy(r, h, eng):
-            if r not in xg:
-                xg[r] = ring4.tile([P, RT * D], BF16, name="xg", align_bytes=64)
-            dst = xg[r][:].bitcast(F32)[:, 512 * h : 512 * (h + 1)].rearrange("p (j r u) -> p j r u", j=2, r=P, u=2)
-            src = tp[(r, h)][:].rearrange("p (j u r) -> p j r u", j=2, u=2, r=P)
-            if eng == "S":
+        def transpose_x(r, half):
+            bank = x_banks.tile([P, BANK], F32, name="x_bank")
+            x_bank[(r, half)] = bank
+            words = x_sb[r][:].bitcast(F32)
+            for j in range(2):
+                for u in range(2):
+                    first = (2 * half + j) * (D // 2) + u * P
+                    place = (2 * j + u) * P
+                    nc.tensor.transpose(bank[:, place : place + P], words[:, first : first + P], identity[:])
+
+        def copy_x(r, half):
+            if half == 0:
+                x_values[r] = ring.tile([P, ROUND * D], BF16, name="x_values", align_bytes=64)
+            dst = x_values[r][:].bitcast(F32)[:, BANK * half : BANK * (half + 1)]
+            dst = dst.rearrange("p (j r u) -> p j r u", j=2, r=P, u=2)
+            src = x_bank[(r, half)][:].rearrange("p (j u r) -> p j r u", j=2, u=2, r=P)
+            if x_copy_engine(r) == "scalar":
                 nc.scalar.copy(out=dst, in_=src)
             else:
                 nc.vector.tensor_copy(out=dst, in_=src)
 
-        def quant(words, plane, values, k, parts):
-            w = RT * P // parts
-            nc.vector.quantize_mx(
-                out=words[:, k * w : (k + 1) * w].bitcast(FP8X4),
-                scales=plane[:, k * w : (k + 1) * w],
-                in_=values[:, 4 * k * w : 4 * (k + 1) * w],
-            )
-
-        def x_quant(r, k):
-            if r not in xq:
-                xq[r] = ring5.tile([P, RT * P], U32, name="xq", align_bytes=64)
-                xc[r] = ring5.tile([P, RT * P], U8, name="xc", align_bytes=64)
-            quant(xq[r], xc[r], xg[r], k, x_parts(r))
+        def quantise_x(r, part):
+            if part == 0:
+                x_words[r] = ring.tile([P, ROUND * P], U32, name="x_words", align_bytes=64)
+                x_scales[r] = ring.tile([P, ROUND * P], U8, name="x_scales", align_bytes=64)
+            quantise_part(x_words[r], x_scales[r], x_values[r], part, x_quantise_parts(r))
 
         def layer1(r, j):
-            bank = hpool.tile([P, 512], F32, name="hp")
-            hp[(r, j)] = bank
-            tok = slice(j * P, (j + 1) * P)
+            bank = h_banks.tile([P, BANK], F32, name="h_bank")
+            h_bank[(r, j)] = bank
+            tokens = slice(j * P, (j + 1) * P)
             for q in range(4):
-                cols = slice(q * P, (q + 1) * P)
+                quarter = slice(q * P, (q + 1) * P)
                 nc.tensor.matmul_mx(
-                    out=bank[:, cols],
-                    lhsT=w1q[:, cols].bitcast(FP8X4),
-                    lhsT_scale=w1s[:, cols],
-                    rhs=xq[r][:, tok].bitcast(FP8X4),
-                    rhs_scale=xc[r][:, tok],
+                    out=bank[:, quarter],
+                    lhsT=w1_words[:, quarter].bitcast(FP8X4),
+                    lhsT_scale=w1_scales[:, quarter],
+                    rhs=x_words[r][:, tokens].bitcast(FP8X4),
+                    rhs_scale=x_scales[r][:, tokens],
                     start=True,
                     stop=True,
                 )
 
-        def h_copy(r, j, eng):
-            if r not in hg:
-                hg[r] = ring4.tile([P, RT * F], BF16, name="hg", align_bytes=64)
-            dst = hg[r][:, j * F : (j + 1) * F].rearrange("p (r t) -> p r t", t=4)
-            src = hp[(r, j)][:].rearrange("p (t r) -> p r t", t=4)
-            relu_out(eng, dst, src)
+        def copy_h(r, j):
+            if j == 0:
+                h_values[r] = ring.tile([P, ROUND * F], BF16, name="h_values", align_bytes=64)
+            relu_out_of_psum(
+                h_copy_engine(r, j),
+                h_values[r][:, j * F : (j + 1) * F].rearrange("p (r t) -> p r t", t=PACK),
+                h_bank[(r, j)][:].rearrange("p (t r) -> p r t", t=PACK),
+            )
 
-        def h_quant(r, k):
-            if r not in hq:
-                hq[r] = ring4.tile([P, RT * P], U32, name="hq", align_bytes=64)
-                hc[r] = ring4.tile([P, RT * P], U8, name="hc", align_bytes=64)
-            quant(hq[r], hc[r], hg[r], k, h_parts(r))
+        def quantise_h(r, part):
+            if part == 0:
+                h_words[r] = ring.tile([P, ROUND * P], U32, name="h_words", align_bytes=64)
+                h_scales[r] = ring.tile([P, ROUND * P], U8, name="h_scales", align_bytes=64)
+            quantise_part(h_words[r], h_scales[r], h_values[r], part, h_quantise_parts(r))
 
-        def layer2(r, h):
-            bank = opool.tile([P, 512], F32, name="op")
-            op[(r, h)] = bank
-            for jl in range(2):
-                tok = slice((2 * h + jl) * P, (2 * h + jl + 1) * P)
+        def layer2(r, half):
+            bank = out_banks.tile([P, BANK], F32, name="out_bank")
+            out_bank[(r, half)] = bank
+            for j in range(2):
+                tokens = slice((2 * half + j) * P, (2 * half + j + 1) * P)
                 nc.tensor.matmul_mx(
-                    out=bank[:, jl * N : (jl + 1) * N],
-                    lhsT=hq[r][:, tok].bitcast(FP8X4),
-                    lhsT_scale=hc[r][:, tok],
-                    rhs=w2q[:].bitcast(FP8X4),
-                    rhs_scale=w2s[:],
+                    out=bank[:, j * N : (j + 1) * N],
+                    lhsT=h_words[r][:, tokens].bitcast(FP8X4),
+                    lhsT_scale=h_scales[r][:, tokens],
+                    rhs=w2_words[:].bitcast(FP8X4),
+                    rhs_scale=w2_scales[:],
                     start=True,
                     stop=True,
                 )
 
-        def o_copy(r, h, eng):
-            relu_out(eng, ob[r][:, 512 * h : 512 * (h + 1)], op[(r, h)][:])
+        def copy_out(r, half):
+            relu_out_of_psum(
+                out_copy_engine(r, half), out_sb[r][:, BANK * half : BANK * (half + 1)], out_bank[(r, half)][:]
+            )
 
-        def store(r, k):
-            w = RT * N // s_parts(r)
-            nc.sync.dma_start(out=ov[:, r * RT * N + k * w : r * RT * N + (k + 1) * w], in_=ob[r][:, k * w : (k + 1) * w])
+        def store(r, part):
+            w = ROUND * N // store_parts(r)
+            first = r * ROUND * N + part * w
+            nc.sync.dma_start(out=out_rows[:, first : first + w], in_=out_sb[r][:, part * w : (part + 1) * w])
 
-        for what, r, i, eng in PLAN:
-            if what == "W1G":
-                w1_mask(r)
-            elif what == "W1Q":
-                w1_quant()
-            elif what == "W2G":
-                w2_mask()
-            elif what == "W2Q":
-                w2_quant()
-            elif what == "T":
-                transposes(r, i)
-            elif what == "XC":
-                x_copy(r, i, eng)
-            elif what == "XQ":
-                x_quant(r, i)
-            elif what == "L1":
-                layer1(r, i)
-            elif what == "HC":
-                h_copy(r, i, eng)
-            elif what == "HQ":
-                h_quant(r, i)
-            elif what == "L2":
-                layer2(r, i)
-            elif what == "OC":
-                o_copy(r, i, eng)
-            else:
-                store(r, i)
+        def live(r):
+            return 0 <= r < ROUNDS
+
+        for q in range(4):
+            mask_w1_quarter(q)
+        for s in range(-AHEAD, ROUNDS + BEHIND):
+            if live(s - BEHIND):
+                for part in range(h_quantise_parts(s - BEHIND)):
+                    quantise_h(s - BEHIND, part)
+            if live(s + AHEAD - 1):
+                for half in range(2):
+                    copy_x(s + AHEAD - 1, half)
+            if s == 1 - AHEAD:
+                quantise_x(0, 0)
+                quantise_w1()
+                quantise_x(0, 1)
+            if s == 0:
+                mask_w2()
+            if live(s) and live(s + 1):
+                quantise_x(s + 1, 0)
+            if s == 0:
+                quantise_w2()
+            if live(s):
+                for j in range(ROUND):
+                    layer1(s, j)
+                for j in range(ROUND):
+                    copy_h(s, j)
+            if live(s - BEHIND):
+                for half in range(2):
+                    layer2(s - BEHIND, half)
+                for half in range(2):
+                    copy_out(s - BEHIND, half)
+                for part in range(store_parts(s - BEHIND)):
+                    store(s - BEHIND, part)
+            if live(s + AHEAD):
+                for half in range(2):
+                    transpose_x(s + AHEAD, half)

@@ -63,9 +63,7 @@ def tile_sparse_connect_t_kernel(tc, x, th1, sign1, th2, sign2, relu, out):
         ctx.enter_context(tc.manual_schedule())
         keep = ctx.enter_context(tc.tile_pool(name="keep", bufs=1))
         ring = ctx.enter_context(tc.tile_pool(name="ring", bufs=4))
-        x_banks = ctx.enter_context(tc.psum_pool(name="x_banks", bufs=2))
-        h_banks = ctx.enter_context(tc.psum_pool(name="h_banks", bufs=4))
-        out_banks = ctx.enter_context(tc.psum_pool(name="out_banks", bufs=2))
+        banks = ctx.enter_context(tc.psum_pool(name="banks", bufs=8))
 
         th1_sb = keep.tile([P, PACK * F], BF16, name="th1_sb")
         sign1_sb = keep.tile([P, PACK * F], BF16, name="sign1_sb")
@@ -160,7 +158,7 @@ def tile_sparse_connect_t_kernel(tc, x, th1, sign1, th2, sign2, relu, out):
             )
 
         def transpose_x(r, half):
-            bank = x_banks.tile([P, BANK], F32, name="x_bank")
+            bank = banks.tile([P, BANK], F32, name="bank")
             x_bank[(r, half)] = bank
             words = x_sb[r][:].bitcast(F32)
             for j in range(2):
@@ -187,7 +185,7 @@ def tile_sparse_connect_t_kernel(tc, x, th1, sign1, th2, sign2, relu, out):
             quantise_part(x_words[r], x_scales[r], x_values[r], part, x_quantise_parts(r))
 
         def layer1(r, j):
-            bank = h_banks.tile([P, BANK], F32, name="h_bank")
+            bank = banks.tile([P, BANK], F32, name="bank")
             h_bank[(r, j)] = bank
             tokens = slice(j * P, (j + 1) * P)
             for q in range(4):
@@ -218,7 +216,7 @@ def tile_sparse_connect_t_kernel(tc, x, th1, sign1, th2, sign2, relu, out):
             quantise_part(h_words[r], h_scales[r], h_values[r], part, h_quantise_parts(r))
 
         def layer2(r, half):
-            bank = out_banks.tile([P, BANK], F32, name="out_bank")
+            bank = banks.tile([P, BANK], F32, name="bank")
             out_bank[(r, half)] = bank
             for j in range(2):
                 tokens = slice((2 * half + j) * P, (2 * half + j + 1) * P)

from contextlib import ExitStack

import concourse.masks as masks
import concourse.mybir as mybir

F32 = mybir.dt.float32
BF16 = mybir.dt.bfloat16
U32 = mybir.dt.uint32
U8 = mybir.dt.uint8
FP8X4 = mybir.dt.float8_e4m3fn_x4
ALU = mybir.AluOpType
ACT = mybir.ActivationFunctionType

P = 128
PACK = 4
TOKENS = 8192
D = 512
F = 512
N = 256
BANK = 512
TILES = TOKENS // P
ROUND = 4
ROUNDS = TILES // ROUND
AHEAD = 3
BEHIND = 2

FLOPS = 2 * TOKENS * D * (F + N)


def x_copy_engine(r):
    return "scalar" if r < AHEAD else "vector"


def h_copy_engine(r, j):
    return "vector" if (r, j) in ((ROUNDS - 2, 1), (ROUNDS - 2, 2), (ROUNDS - 1, 0), (ROUNDS - 1, 1)) else "scalar"


def out_copy_engine(r, half):
    if half == 0 or r in (4, ROUNDS - 4, ROUNDS - 3, ROUNDS - 2):
        return "scalar"
    return "vector"


def x_quantise_parts(r):
    return 2 if r == 0 else 1


def h_quantise_parts(r):
    return 2 if r >= ROUNDS - 2 else 1


def store_parts(r):
    return 2 if r >= ROUNDS - 3 else 1


def tile_sparse_connect_t_kernel(tc, x, th1, sign1, th2, sign2, relu, out):
    assert relu == 1
    nc = tc.nc
    x_rows = x.flatten_outer_dims().rearrange("(p j) k -> p (j k)", j=TILES)
    out_rows = out.flatten_outer_dims().rearrange("(p j) n -> p (j n)", j=TILES)

    with ExitStack() as ctx:
        ctx.enter_context(tc.manual_schedule())
        keep = ctx.enter_context(tc.tile_pool(name="keep", bufs=1))
        ring = ctx.enter_context(tc.tile_pool(name="ring", bufs=4))
        banks = ctx.enter_context(tc.psum_pool(name="banks", bufs=8))

        th1_sb = keep.tile([P, PACK * F], BF16, name="th1_sb")
        sign1_sb = keep.tile([P, PACK * F], BF16, name="sign1_sb")
        th2_sb = keep.tile([P, PACK * N], BF16, name="th2_sb")
        sign2_sb = keep.tile([P, PACK * N], BF16, name="sign2_sb")
        x_sb = [keep.tile([P, ROUND * D], BF16, name="x_sb%d" % r) for r in range(ROUNDS)]
        out_sb = [keep.tile([P, ROUND * N], F32, name="out_sb%d" % r) for r in range(ROUNDS)]

        def load_w1(dst, src):
            nc.sync.dma_start(
                out=dst[:].rearrange("p (u c) -> p u c", u=2),
                in_=src.rearrange("(u p e) f -> p u (e f)", u=2, p=P, e=2),
            )

        def load_w2(dst, src):
            nc.sync.dma_start(out=dst[:], in_=src.rearrange("(p t) n -> p (t n)", t=PACK))

        def load_x(r):
            nc.sync.dma_start(out=x_sb[r][:], in_=x_rows[:, r * ROUND * D : (r + 1) * ROUND * D])

        load_w1(th1_sb, th1)
        load_w1(sign1_sb, sign1)
        for r in range(AHEAD):
            load_x(r)
        load_w2(th2_sb, th2)
        load_w2(sign2_sb, sign2)
        for r in range(AHEAD, ROUNDS):
            load_x(r)

        identity = keep.tile([P, P], F32, name="identity")
        masks.make_identity(nc, identity[:])
        warm_in = keep.tile([P, 1], F32, name="warm_in")
        warm_out = keep.tile([P, 1], F32, name="warm_out")
        nc.vector.memset(warm_in[:], 0.0)
        nc.scalar.activation(out=warm_out[:], in_=warm_in[:], func=ACT.Relu)

        w1_values = keep.tile([P, PACK * F], BF16, name="w1_values", align_bytes=64)
        w1_words = keep.tile([P, F], U32, name="w1_words", align_bytes=64)
        w1_scales = keep.tile([P, F], U8, name="w1_scales", align_bytes=64)
        w2_values = keep.tile([P, PACK * N], BF16, name="w2_values", align_bytes=64)
        w2_words = keep.tile([P, N], U32, name="w2_words", align_bytes=64)
        w2_scales = keep.tile([P, N], U8, name="w2_scales", align_bytes=64)

        def mask_w1_quarter(q):
            nc.vector.scalar_tensor_tensor(
                out=w1_values[:].rearrange("p (q m t) -> p q m t", q=4, m=P, t=PACK)[:, q],
                in0=th1_sb[:].rearrange("p (t m q) -> p q m t", t=PACK, m=P, q=4)[:, q],
                scalar=0.0,
                in1=sign1_sb[:].rearrange("p (t m q) -> p q m t", t=PACK, m=P, q=4)[:, q],
                op0=ALU.max,
                op1=ALU.mult,
            )

        def quantise_w1():
            nc.vector.quantize_mx(out=w1_words[:].bitcast(FP8X4), scales=w1_scales[:], in_=w1_values[:])

        def mask_w2():
            nc.vector.scalar_tensor_tensor(
                out=w2_values[:].rearrange("p (n t) -> p n t", t=PACK),
                in0=th2_sb[:].rearrange("p (t n) -> p n t", t=PACK),
                scalar=0.0,
                in1=sign2_sb[:].rearrange("p (t n) -> p n t", t=PACK),
                op0=ALU.max,
                op1=ALU.mult,
            )

        def quantise_w2():
            nc.vector.quantize_mx(out=w2_words[:].bitcast(FP8X4), scales=w2_scales[:], in_=w2_values[:])

        x_bank = {}
        x_values = {}
        x_words = {}
        x_scales = {}
        h_bank = {}
        h_values = {}
        h_words = {}
        h_scales = {}
        out_bank = {}

        def relu_out_of_psum(engine, dst, src):
            if engine == "scalar":
                nc.scalar.activation(out=dst, in_=src, func=ACT.Relu)
            else:
                nc.vector.tensor_scalar_max(out=dst, in0=src, scalar1=0.0)

        def quantise_part(words, scales, values, part, parts):
            w = ROUND * P // parts
            nc.vector.quantize_mx(
                out=words[:, part * w : (part + 1) * w].bitcast(FP8X4),
                scales=scales[:, part * w : (part + 1) * w],
                in_=values[:, PACK * part * w : PACK * (part + 1) * w],
            )

        def transpose_x(r, half):
            bank = banks.tile([P, BANK], F32, name="bank")
            x_bank[(r, half)] = bank
            words = x_sb[r][:].bitcast(F32)
            for j in range(2):
                for u in range(2):
                    first = (2 * half + j) * (D // 2) + u * P
                    place = (2 * j + u) * P
                    nc.tensor.transpose(bank[:, place : place + P], words[:, first : first + P], identity[:])

        def copy_x(r, half):
            if half == 0:
                x_values[r] = ring.tile([P, ROUND * D], BF16, name="x_values", align_bytes=64)
            dst = x_values[r][:].bitcast(F32)[:, BANK * half : BANK * (half + 1)]
            dst = dst.rearrange("p (j r u) -> p j r u", j=2, r=P, u=2)
            src = x_bank[(r, half)][:].rearrange("p (j u r) -> p j r u", j=2, u=2, r=P)
            if x_copy_engine(r) == "scalar":
                nc.scalar.copy(out=dst, in_=src)
            else:
                nc.vector.tensor_copy(out=dst, in_=src)

        def quantise_x(r, part):
            if part == 0:
                x_words[r] = ring.tile([P, ROUND * P], U32, name="x_words", align_bytes=64)
                x_scales[r] = ring.tile([P, ROUND * P], U8, name="x_scales", align_bytes=64)
            quantise_part(x_words[r], x_scales[r], x_values[r], part, x_quantise_parts(r))

        def layer1(r, j):
            bank = banks.tile([P, BANK], F32, name="bank")
            h_bank[(r, j)] = bank
            tokens = slice(j * P, (j + 1) * P)
            for q in range(4):
                quarter = slice(q * P, (q + 1) * P)
                nc.tensor.matmul_mx(
                    out=bank[:, quarter],
                    lhsT=w1_words[:, quarter].bitcast(FP8X4),
                    lhsT_scale=w1_scales[:, quarter],
                    rhs=x_words[r][:, tokens].bitcast(FP8X4),
                    rhs_scale=x_scales[r][:, tokens],
                    start=True,
                    stop=True,
                )

        def copy_h(r, j):
            if j == 0:
                h_values[r] = ring.tile([P, ROUND * F], BF16, name="h_values", align_bytes=64)
            relu_out_of_psum(
                h_copy_engine(r, j),
                h_values[r][:, j * F : (j + 1) * F].rearrange("p (r t) -> p r t", t=PACK),
                h_bank[(r, j)][:].rearrange("p (t r) -> p r t", t=PACK),
            )

        def quantise_h(r, part):
            if part == 0:
                h_words[r] = ring.tile([P, ROUND * P], U32, name="h_words", align_bytes=64)
                h_scales[r] = ring.tile([P, ROUND * P], U8, name="h_scales", align_bytes=64)
            quantise_part(h_words[r], h_scales[r], h_values[r], part, h_quantise_parts(r))

        def layer2(r, half):
            bank = banks.tile([P, BANK], F32, name="bank")
            out_bank[(r, half)] = bank
            for j in range(2):
                tokens = slice((2 * half + j) * P, (2 * half + j + 1) * P)
                nc.tensor.matmul_mx(
                    out=bank[:, j * N : (j + 1) * N],
                    lhsT=h_words[r][:, tokens].bitcast(FP8X4),
                    lhsT_scale=h_scales[r][:, tokens],
                    rhs=w2_words[:].bitcast(FP8X4),
                    rhs_scale=w2_scales[:],
                    start=True,
                    stop=True,
                )

        def copy_out(r, half):
            relu_out_of_psum(
                out_copy_engine(r, half), out_sb[r][:, BANK * half : BANK * (half + 1)], out_bank[(r, half)][:]
            )

        def store(r, part):
            w = ROUND * N // store_parts(r)
            first = r * ROUND * N + part * w
            nc.sync.dma_start(out=out_rows[:, first : first + w], in_=out_sb[r][:, part * w : (part + 1) * w])

        def live(r):
            return 0 <= r < ROUNDS

        for q in range(4):
            mask_w1_quarter(q)
        for s in range(-AHEAD, ROUNDS + BEHIND):
            if live(s - BEHIND):
                for part in range(h_quantise_parts(s - BEHIND)):
                    quantise_h(s - BEHIND, part)
            if live(s + AHEAD - 1):
                for half in range(2):
                    copy_x(s + AHEAD - 1, half)
            if s == 1 - AHEAD:
                quantise_x(0, 0)
                quantise_w1()
                quantise_x(0, 1)
            if s == 0:
                mask_w2()
            if live(s) and live(s + 1):
                quantise_x(s + 1, 0)
            if s == 0:
                quantise_w2()
            if live(s):
                for j in range(ROUND):
                    layer1(s, j)
                for j in range(ROUND):
                    copy_h(s, j)
            if live(s - BEHIND):
                for half in range(2):
                    layer2(s - BEHIND, half)
                for half in range(2):
                    copy_out(s - BEHIND, half)
                for part in range(store_parts(s - BEHIND)):
                    store(s - BEHIND, part)
            if live(s + AHEAD):
                for half in range(2):
                    transpose_x(s + AHEAD, half)
